import numpy as np
import ml_dtypes


def mxq(x, axis, fmt="e4m3"):
    dtype, down = {"e4m3": (ml_dtypes.float8_e4m3fn, 7), "e5m2": (ml_dtypes.float8_e5m2, 14)}[fmt]
    v = np.moveaxis(np.asarray(x, np.float32).astype(ml_dtypes.bfloat16).astype(np.float64), axis, -1)
    blocks = v.reshape(v.shape[:-1] + (-1, 32))
    amax = np.abs(blocks).max(-1, keepdims=True)
    byte = np.maximum(np.where(amax > 0, np.frexp(amax)[1] - 1 + 127, 0) - down, 1)
    scale = np.exp2(byte - 127.0)
    codes = (blocks / scale).astype(np.float32).astype(dtype).astype(np.float64)
    return np.moveaxis((codes * scale).reshape(v.shape), -1, axis)


WIDE = False


def mx_kscale(k):
    if not WIDE:
        return np.ones(k)
    levels = np.array([10, -10, 5, -5, 0])
    if k % 512:
        return np.exp2(np.random.permutation(np.resize(levels, k // 32))).repeat(32)
    a = np.empty((k // 512, 16))
    for p in range(k // 512):
        a[p, :8] = np.random.permutation(np.resize(levels, 8))
        for g in range(8):
            far = levels[np.abs(levels - a[p, g]) >= 10]
            a[p, g + 8] = far[np.random.randint(len(far))]
    return np.exp2(a.ravel()).repeat(32)


BF16 = ml_dtypes.bfloat16


def bf(x):
    return np.asarray(x, np.float32).astype(BF16)


def f64(x):
    return np.asarray(x).astype(np.float64)


B, N, W, H, D = 1, 4, 512, 2, 512


def setup_inputs():
    s = mx_kscale(D)
    u = mx_kscale(D)
    m = np.random.uniform(0.2, 1.0, (N, N))
    k0 = bf(np.maximum(np.random.standard_normal((B, H, N, W, D)) * 0.5, 0.0))
    v0 = bf(np.random.standard_normal((B, H, N, W, D)) * 0.5)
    g = np.random.standard_normal((B, H, N, D, D)) * np.exp2(np.random.randint(-6, 1, (B, H, N, D, 1)))
    return {"k_feat": bf(f64(k0) * s),
            "v": bf(f64(v0) / u),
            "w_piece": bf(m / m.sum(axis=0, keepdims=True)),
            "grad_out": bf(g / s[:, None] * u)}


def reference(k_feat, v, w_piece, grad_out):
    wp = f64(w_piece)
    g = f64(grad_out)
    dkv = (wp[None, None, :, :, None, None] * g[:, :, :, None, :, :]).sum(axis=2)
    dk = mxq(f64(v), 4, "e4m3") @ mxq(dkv, 4, "e5m2").transpose(0, 1, 2, 4, 3)
    dv = mxq(f64(k_feat), 4, "e4m3") @ mxq(dkv, 3, "e5m2")
    return dk, dv

@@ -1,0 +1,293 @@
+from contextlib import ExitStack
+
+import concourse.mybir as mybir
+from concourse.masks import make_identity
+
+F32 = mybir.dt.float32
+BF16 = mybir.dt.bfloat16
+U32 = mybir.dt.uint32
+U8 = mybir.dt.uint8
+E4M3 = mybir.dt.float8_e4m3fn_x4
+E5M2 = mybir.dt.float8_e5m2_x4
+MULT = mybir.AluOpType.mult
+ADD = mybir.AluOpType.add
+
+H, N, W, D = 2, 4, 512, 512
+P = 128
+PAIRS = H * N
+FLOPS = 2 * 2 * PAIRS * W * D * D
+
+
+def tile_mhla_pa_v_kernel(tc, k_feat, v, w_piece, grad_out, out_0, out_1):
+    nc = tc.nc
+    with ExitStack() as ctx:
+        const = ctx.enter_context(tc.tile_pool(name="const", bufs=1))
+        keep = ctx.enter_context(tc.tile_pool(name="keep", bufs=1))
+        work = ctx.enter_context(tc.tile_pool(name="work", bufs=2))
+        psum = ctx.enter_context(tc.psum_pool(name="psum", bufs=8))
+
+        w_all = const.tile([P, 16], BF16, name="w_all")
+        nc.scalar.dma_start(out=w_all[:], in_=w_piece.rearrange("i j -> (i j)").partition_broadcast(P))
+
+        ident = const.tile([P, P], BF16, name="ident")
+        make_identity(nc, ident[:])
+        ident_f = const.tile([P, P], F32, name="ident_f")
+        make_identity(nc, ident_f[:])
+
+        raw = {}
+        g_mix = {}
+        g_row = {}
+
+        def load_kv(which, n):
+            h, j = divmod(n, N)
+            t = keep.tile([P, 2048], BF16, name=which + str(n), align_bytes=64)
+            src = (k_feat if which == "k" else v)[0, h, j].rearrange("(m b) d -> m (b d)", b=4)
+            nc.sync.dma_start(out=t[:], in_=src)
+            raw[which, n] = t
+
+        def load_rows(h):
+            t = keep.tile([P, N, 512], BF16, name="g_row" + str(h), align_bytes=64)
+            src = grad_out[0, h].rearrange("i (q s) d -> q i s d", s=4)
+            nc.sync.dma_start(out=t[:], in_=src[:, :, 3, :])
+            g_row[h] = t
+
+        def load_mix(h, half):
+            if half == 0:
+                g_mix[h] = keep.tile([P, 4, 1536], BF16, name="g_mix" + str(h), align_bytes=64)
+            for i in range(N):
+                src = grad_out[0, h, i].rearrange("(q r s) d -> r q (s d)", q=4, s=4)
+                nc.sync.dma_start(
+                    out=g_mix[h][32 * i : 32 * i + 32, 2 * half : 2 * half + 2, :],
+                    in_=src[:, 2 * half : 2 * half + 2, 0:1536],
+                )
+
+        load_rows(0)
+        load_kv("v", 0)
+        load_mix(0, 0)
+        load_mix(0, 1)
+        load_kv("k", 0)
+        load_kv("v", 1)
+        load_kv("k", 1)
+        load_mix(1, 0)
+        load_mix(1, 1)
+        load_rows(1)
+        for n in range(2, PAIRS):
+            load_kv("v", n)
+            load_kv("k", n)
+
+        warm = const.tile([P, 1], F32, name="warm")
+        nc.vector.memset(warm[:], 0.0)
+        nc.scalar.copy(out=warm[:], in_=warm[:])
+        w_f = const.tile([P, 16], F32, name="w_f")
+        nc.vector.tensor_copy(out=w_f[:], in_=w_all[:])
+        w_col = const.tile([P, N], F32, name="w_col")
+        eye = const.tile([P, 32], BF16, name="eye")
+        for i in range(4):
+            quad = slice(32 * i, 32 * i + 32)
+            nc.vector.tensor_copy(out=w_col[quad, :], in_=w_all[quad, 4 * i : 4 * i + 4])
+            nc.vector.tensor_copy(out=eye[quad, :], in_=ident[quad, quad])
+        mixer = const.tile([P, P], BF16, name="mixer", align_bytes=64)
+        for j in range(N):
+            nc.vector.tensor_scalar(
+                out=mixer[:, 32 * j : 32 * j + 32], in0=eye[:], scalar1=w_col[:, j : j + 1], scalar2=None, op0=MULT
+            )
+
+        b_in = [keep.tile([P, N, 512, 4], BF16, name="b_in" + str(h), align_bytes=64) for h in range(H)]
+        acc = {}
+        row = {}
+        a_in = {}
+        grouped = {}
+        codes = {}
+        load = {"v": 0, "s": 0}
+
+        def copy_out(dst, src, columns):
+            cost = 830 * columns // 1000 + 60
+            if load["v"] < load["s"]:
+                load["v"] += cost
+                nc.vector.tensor_copy(out=dst, in_=src)
+            else:
+                load["s"] += cost + 0
+                nc.scalar.copy(out=dst, in_=src)
+
+        def f32_bank():
+            return psum.tile([P, 512], F32, name="bank")
+
+        def bf16_bank():
+            return psum.tile([P, 1024], BF16, name="bank")
+
+        def mix(n, i):
+            if n >= PAIRS:
+                return
+            h, j = divmod(n, N)
+            w_ij = w_f[:, 4 * i + j : 4 * i + j + 1]
+            if i == 0:
+                acc[n] = work.tile([P, 512], F32, name="acc", bufs=3)
+                load["v"] += 230
+                nc.vector.tensor_scalar(out=acc[n][:], in0=g_row[h][:, 0, :], scalar1=w_ij, scalar2=None, op0=MULT)
+                return
+            if i == 3:
+                row[n] = work.tile([P, 512], BF16, name="row", bufs=3, align_bytes=64)
+            dst = row[n] if i == 3 else acc[n]
+            load["v"] += 480
+            nc.vector.scalar_tensor_tensor(
+                out=dst[:], in0=g_row[h][:, i, :], scalar=w_ij, in1=acc[n][:], op0=MULT, op1=ADD
+            )
+
+        def spread_rows(n):
+            if n >= PAIRS:
+                return
+            h, j = divmod(n, N)
+            bank = bf16_bank()
+            for t in range(4):
+                nc.tensor.transpose(bank[:, 128 * t : 128 * t + 128], row[n][:, t:512:4], ident[:])
+            copy_out(b_in[h][:, j, 384:512, :], bank[:, 0:512].rearrange("p (t q) -> p q t", t=4), 512)
+
+        def kron(h, s, half):
+            bank = bf16_bank()
+            view = bank[:].rearrange("p (g t c) -> p g t c", g=2, t=4)
+            for g in range(2):
+                for t in range(4):
+                    nc.tensor.matmul(
+                        view[:, g, t, :],
+                        lhsT=g_mix[h][:, 2 * half + g, 512 * s + t : 512 * s + 512 : 4],
+                        rhs=mixer[:],
+                        start=True,
+                        stop=True,
+                    )
+            for g in range(2):
+                c0 = 128 * s + 64 * half + 32 * g
+                copy_out(b_in[h][:, :, c0 : c0 + 32, :], view[:, g].rearrange("p t (j r) -> p j r t", j=4), 512)
+
+        def turn(which, n, half):
+            if n >= PAIRS:
+                return
+            if half == 0:
+                grouped[which, n] = work.tile([P, 2048], BF16, name="grouped_" + which, align_bytes=64)
+            words = raw[which, n][:].bitcast(F32)
+            bank = f32_bank()
+            for b in range(2):
+                for u in range(2):
+                    w0 = 256 * (2 * half + b)
+                    nc.tensor.transpose(
+                        bank[:, 256 * b + 128 * u : 256 * b + 128 * u + 128], words[:, w0 + u : w0 + 256 : 2], ident_f[:]
+                    )
+            dst = grouped[which, n][:].bitcast(F32)[:, 512 * half : 512 * half + 512]
+            copy_out(
+                dst.rearrange("p (b m u) -> p b m u", b=2, u=2),
+                bank[:].rearrange("p (b u m) -> p b m u", b=2, u=2),
+                512,
+            )
+
+        def quant(which, n):
+            if n >= PAIRS:
+                return
+            h, j = divmod(n, N)
+            if which == "b":
+                src, fmt = b_in[h][:, j].rearrange("p c t -> p (c t)"), E5M2
+            elif which == "a":
+                src, fmt = a_in[n][:], E5M2
+            else:
+                src, fmt = grouped[which, n][:], E4M3
+            c = work.tile([P, 512], U32, name="codes_" + which, align_bytes=64)
+            sc = work.tile([P, 512], U8, name="scales_" + which, align_bytes=64)
+            load["v"] += 480
+            nc.vector.quantize_mx(out=c[:].bitcast(fmt), scales=sc[:], in_=src)
+            codes[which, n] = (c, sc)
+
+        def back(n, half):
+            if n >= PAIRS:
+                return
+            h, j = divmod(n, N)
+            if half == 0:
+                a_in[n] = work.tile([P, 2048], BF16, name="a_in", align_bytes=64)
+            bank = bf16_bank()
+            for tt in range(2):
+                for s in range(4):
+                    c0 = 512 * tt + 128 * s
+                    nc.tensor.transpose(
+                        bank[:, c0 : c0 + 128], b_in[h][:, j, 128 * s : 128 * s + 128, 2 * half + tt], ident[:]
+                    )
+            for tt in range(2):
+                dst = a_in[n][:, 1024 * half + 512 * tt : 1024 * half + 512 * tt + 512]
+                copy_out(
+                    dst.rearrange("q (p s) -> q p s", s=4),
+                    bank[:, 512 * tt : 512 * tt + 512].rearrange("q (s p) -> q p s", s=4),
+                    512,
+                )
+
+        def product(n, which):
+            if n >= PAIRS:
+                return
+            h, j = divmod(n, N)
+            left, right, dram = ("v", "b", out_0) if which == 0 else ("k", "a", out_1)
+            lc, ls = codes[left, n]
+            rc, rs = codes[right, n]
+            res = work.tile([P, 4, 512], F32, name="res" + str(which))
+            view = dram[0, h, j].rearrange("(m b) d -> m b d", b=4)
+            last = n == PAIRS - 1
+            for b in range(4):
+                bank = f32_bank()
+                cols = slice(128 * b, 128 * b + 128)
+                nc.tensor.matmul_mx(
+                    out=bank[:],
+                    lhsT=lc[:, cols].bitcast(E4M3),
+                    lhsT_scale=ls[:, cols],
+                    rhs=rc[:].bitcast(E5M2),
+                    rhs_scale=rs[:],
+                    start=True,
+                    stop=True,
+                )
+                copy_out(
+                    res[:, b, :].rearrange("m (q s) -> m q s", s=4), bank[:].rearrange("m (s q) -> m q s", s=4), 512
+                )
+                if last and which == 1:
+                    nc.sync.dma_start(out=view[:, b, :], in_=res[:, b, :])
+                elif b % 2 == 1:
+                    nc.sync.dma_start(out=view[:, b - 1 : b + 1, :], in_=res[:, b - 1 : b + 1, :])
+
+        with tc.manual_schedule():
+            units = [(s, half) for half in range(2) for s in range(3)]
+            turn("v", 0, 0)
+            turn("v", 0, 1)
+            for i in range(N):
+                mix(0, i)
+            for s, half in units[0:3]:
+                kron(0, s, half)
+            quant("v", 0)
+            for s, half in units[3:6]:
+                kron(0, s, half)
+            spread_rows(0)
+            quant("b", 0)
+            back(0, 0)
+            back(0, 1)
+            mix(1, 0)
+            mix(1, 1)
+            product(0, 0)
+            turn("k", 0, 0)
+            turn("k", 0, 1)
+            mix(1, 2)
+            quant("a", 0)
+            mix(1, 3)
+            quant("k", 0)
+            spread_rows(1)
+            for n in range(PAIRS):
+                mix(n + 2, 0)
+                back(n + 1, 0)
+                quant("b", n + 1)
+                turn("v", n + 1, 0)
+                turn("v", n + 1, 1)
+                mix(n + 2, 1)
+                product(n, 1)
+                quant("v", n + 1)
+                back(n + 1, 1)
+                mix(n + 2, 2)
+                turn("k", n + 1, 0)
+                turn("k", n + 1, 1)
+                quant("a", n + 1)
+                mix(n + 2, 3)
+                product(n + 1, 0)
+                quant("k", n + 1)
+                if n < 3:
+                    for s, half in units[2 * n : 2 * n + 2]:
+                        kron(1, s, half)
+                spread_rows(n + 2)

@@ -47,22 +47,21 @@ def tile_mhla_pa_v_kernel(tc, k_feat, v, w_piece, grad_out, out_0, out_1):
 
         def load_rows(h):
             t = keep.tile([P, N, 512], BF16, name="g_row" + str(h), align_bytes=64)
-            src = grad_out[0, h].rearrange("i (q s) d -> q i s d", s=4)
-            nc.sync.dma_start(out=t[:], in_=src[:, :, 3, :])
+            nc.sync.dma_start(out=t[:], in_=grad_out[0, h].rearrange("i q d -> q i d")[384:512])
             g_row[h] = t
 
         def load_mix(h, half):
             if half == 0:
-                g_mix[h] = keep.tile([P, 4, 1536], BF16, name="g_mix" + str(h), align_bytes=64)
+                g_mix[h] = keep.tile([P, 12, 512], BF16, name="g_mix" + str(h), align_bytes=64)
             for i in range(N):
-                src = grad_out[0, h, i].rearrange("(q r s) d -> r q (s d)", q=4, s=4)
+                src = grad_out[0, h, i].rearrange("(x r) d -> r x d", r=32)
                 nc.sync.dma_start(
-                    out=g_mix[h][32 * i : 32 * i + 32, 2 * half : 2 * half + 2, :],
-                    in_=src[:, 2 * half : 2 * half + 2, 0:1536],
+                    out=g_mix[h][32 * i : 32 * i + 32, 6 * half : 6 * half + 6, :],
+                    in_=src[:, 6 * half : 6 * half + 6, :],
                 )
 
-        load_rows(0)
         load_kv("v", 0)
+        load_rows(0)
         load_mix(0, 0)
         load_mix(0, 1)
         load_kv("k", 0)
@@ -85,24 +84,33 @@ def tile_mhla_pa_v_kernel(tc, k_feat, v, w_piece, grad_out, out_0, out_1):
         for i in range(4):
             quad = slice(32 * i, 32 * i + 32)
             nc.vector.tensor_copy(out=w_col[quad, :], in_=w_all[quad, 4 * i : 4 * i + 4])
-            nc.vector.tensor_copy(out=eye[quad, :], in_=ident[quad, quad])
+            nc.vector.tensor_copy(
+                out=eye[quad, :].rearrange("p (u q e) -> p q u e", u=2, e=2),
+                in_=ident[quad, quad].rearrange("p (q u e) -> p q u e", u=2, e=2),
+            )
+        perm = const.tile([P, P], BF16, name="perm", align_bytes=64)
+        nc.vector.tensor_copy(
+            out=perm[:].rearrange("p (u q e) -> p q u e", u=2, e=2),
+            in_=ident[:].rearrange("p (q u e) -> p q u e", u=2, e=2),
+        )
         mixer = const.tile([P, P], BF16, name="mixer", align_bytes=64)
         for j in range(N):
             nc.vector.tensor_scalar(
                 out=mixer[:, 32 * j : 32 * j + 32], in0=eye[:], scalar1=w_col[:, j : j + 1], scalar2=None, op0=MULT
             )
 
-        b_in = [keep.tile([P, N, 512, 4], BF16, name="b_in" + str(h), align_bytes=64) for h in range(H)]
+        mixed = [keep.tile([P, 4, N, 512], BF16, name="mixed" + str(h), align_bytes=64) for h in range(H)]
+        b_in = {}
         acc = {}
         row = {}
         a_in = {}
         grouped = {}
         codes = {}
-        load = {"v": 0, "s": 0}
+        load = {"v": 0, "s": 3000}
 
-        def copy_out(dst, src, columns):
+        def copy_out(dst, src, columns, engine=None):
             cost = 830 * columns // 1000 + 60
-            if load["v"] < load["s"]:
+            if engine == "v" or (engine is None and load["v"] < load["s"]):
                 load["v"] += cost
                 nc.vector.tensor_copy(out=dst, in_=src)
             else:
@@ -139,26 +147,39 @@ def tile_mhla_pa_v_kernel(tc, k_feat, v, w_piece, grad_out, out_0, out_1):
             h, j = divmod(n, N)
             bank = bf16_bank()
             for t in range(4):
-                nc.tensor.transpose(bank[:, 128 * t : 128 * t + 128], row[n][:, t:512:4], ident[:])
-            copy_out(b_in[h][:, j, 384:512, :], bank[:, 0:512].rearrange("p (t q) -> p q t", t=4), 512)
+                nc.tensor.transpose(bank[:, 128 * t : 128 * t + 128], row[n][:, t:512:4], perm[:])
+            dst = mixed[h][:, :, j, :].rearrange("p t (u q) -> p t u q", u=2)
+            copy_out(dst[:, :, :, 192:256], bank[:, 0:512].rearrange("p (t u q) -> p t u q", t=4, u=2), 256)
 
-        def kron(h, s, half):
+        def kron(h, x):
             bank = bf16_bank()
-            view = bank[:].rearrange("p (g t c) -> p g t c", g=2, t=4)
             for g in range(2):
                 for t in range(4):
+                    c0 = 512 * g + 128 * t
                     nc.tensor.matmul(
-                        view[:, g, t, :],
-                        lhsT=g_mix[h][:, 2 * half + g, 512 * s + t : 512 * s + 512 : 4],
+                        bank[:, c0 : c0 + 128],
+                        lhsT=g_mix[h][:, 2 * x + g, t:512:4],
                         rhs=mixer[:],
                         start=True,
                         stop=True,
                     )
-            for g in range(2):
-                c0 = 128 * s + 64 * half + 32 * g
-                copy_out(b_in[h][:, :, c0 : c0 + 32, :], view[:, g].rearrange("p t (j r) -> p j r t", j=4), 512)
+            dst = mixed[h][:].rearrange("p t j (u q) -> p (t j u) q", u=2)[:, :, 32 * x : 32 * x + 32]
+            copy_out(
+                dst.rearrange("p a (g y) -> p a g y", g=2), bank[:].rearrange("p (g a y) -> p a g y", g=2, y=16), 512
+            )
 
-        def turn(which, n, half):
+        def interleave(n):
+            if n >= PAIRS:
+                return
+            h, j = divmod(n, N)
+            b_in[n] = work.tile([P, 2048], BF16, name="b_in", align_bytes=64)
+            load["v"] += 1090
+            nc.vector.tensor_copy(
+                out=b_in[n][:].rearrange("p (c i t) -> p c t i", i=4, t=4),
+                in_=mixed[h][:, :, j, :].rearrange("p t (c i) -> p c t i", i=4),
+            )
+
+        def turn(which, n, half, engine=None):
             if n >= PAIRS:
                 return
             if half == 0:
@@ -176,6 +197,7 @@ def tile_mhla_pa_v_kernel(tc, k_feat, v, w_piece, grad_out, out_0, out_1):
                 dst.rearrange("p (b m u) -> p b m u", b=2, u=2),
                 bank[:].rearrange("p (b u m) -> p b m u", b=2, u=2),
                 512,
+                engine,
             )
 
         def quant(which, n):
@@ -183,7 +205,7 @@ def tile_mhla_pa_v_kernel(tc, k_feat, v, w_piece, grad_out, out_0, out_1):
                 return
             h, j = divmod(n, N)
             if which == "b":
-                src, fmt = b_in[h][:, j].rearrange("p c t -> p (c t)"), E5M2
+                src, fmt = b_in[n][:], E5M2
             elif which == "a":
                 src, fmt = a_in[n][:], E5M2
             else:
@@ -200,32 +222,34 @@ def tile_mhla_pa_v_kernel(tc, k_feat, v, w_piece, grad_out, out_0, out_1):
             h, j = divmod(n, N)
             if half == 0:
                 a_in[n] = work.tile([P, 2048], BF16, name="a_in", align_bytes=64)
-            bank = bf16_bank()
+            words = mixed[h][:].rearrange("p t j c -> p (t j c)").bitcast(F32)
+            bank = f32_bank()
             for tt in range(2):
-                for s in range(4):
-                    c0 = 512 * tt + 128 * s
-                    nc.tensor.transpose(
-                        bank[:, c0 : c0 + 128], b_in[h][:, j, 128 * s : 128 * s + 128, 2 * half + tt], ident[:]
-                    )
-            for tt in range(2):
-                dst = a_in[n][:, 1024 * half + 512 * tt : 1024 * half + 512 * tt + 512]
-                copy_out(
-                    dst.rearrange("q (p s) -> q p s", s=4),
-                    bank[:, 512 * tt : 512 * tt + 512].rearrange("q (s p) -> q p s", s=4),
-                    512,
-                )
+                for u in range(2):
+                    c0 = 256 * tt + 128 * u
+                    w0 = 256 * (N * (2 * half + tt) + j) + 128 * u
+                    nc.tensor.transpose(bank[:, c0 : c0 + 128], words[:, w0 : w0 + 128], ident_f[:])
+            dst = a_in[n][:].bitcast(F32)[:, 512 * half : 512 * half + 512]
+            copy_out(
+                dst.rearrange("q (t p u) -> q t p u", t=2, u=2),
+                bank[:].rearrange("q (t u p) -> q t p u", t=2, u=2),
+                512,
+            )
 
-        def product(n, which):
+        results = {}
+
+        def product(n, which, pair):
             if n >= PAIRS:
                 return
             h, j = divmod(n, N)
             left, right, dram = ("v", "b", out_0) if which == 0 else ("k", "a", out_1)
             lc, ls = codes[left, n]
             rc, rs = codes[right, n]
-            res = work.tile([P, 4, 512], F32, name="res" + str(which))
+            if pair == 0:
+                results[which] = work.tile([P, 4, 512], F32, name="res" + str(which))
+            res = results[which]
             view = dram[0, h, j].rearrange("(m b) d -> m b d", b=4)
-            last = n == PAIRS - 1
-            for b in range(4):
+            for b in range(2 * pair, 2 * pair + 2):
                 bank = f32_bank()
                 cols = slice(128 * b, 128 * b + 128)
                 nc.tensor.matmul_mx(
@@ -237,57 +261,63 @@ def tile_mhla_pa_v_kernel(tc, k_feat, v, w_piece, grad_out, out_0, out_1):
                     start=True,
                     stop=True,
                 )
-                copy_out(
-                    res[:, b, :].rearrange("m (q s) -> m q s", s=4), bank[:].rearrange("m (s q) -> m q s", s=4), 512
-                )
-                if last and which == 1:
+                if which == 0:
+                    dst = res[:, b, :].rearrange("m (q u e) -> m q u e", u=2, e=2)
+                    src = bank[:].rearrange("m (u q e) -> m q u e", u=2, e=2)
+                else:
+                    dst = res[:, b, :].rearrange("m (p t) -> m p t", t=4)
+                    src = bank[:].rearrange("m (t p) -> m p t", t=4)
+                copy_out(dst, src, 512)
+                if n == PAIRS - 1 and which == 1:
                     nc.sync.dma_start(out=view[:, b, :], in_=res[:, b, :])
-                elif b % 2 == 1:
-                    nc.sync.dma_start(out=view[:, b - 1 : b + 1, :], in_=res[:, b - 1 : b + 1, :])
+            if not (n == PAIRS - 1 and which == 1):
+                nc.sync.dma_start(out=view[:, 2 * pair : 2 * pair + 2, :], in_=res[:, 2 * pair : 2 * pair + 2, :])
 
         with tc.manual_schedule():
-            units = [(s, half) for half in range(2) for s in range(3)]
-            turn("v", 0, 0)
-            turn("v", 0, 1)
+            turn("v", 0, 0, "s")
+            turn("v", 0, 1, "s")
             for i in range(N):
                 mix(0, i)
-            for s, half in units[0:3]:
-                kron(0, s, half)
+                mix(1, i)
             quant("v", 0)
-            for s, half in units[3:6]:
-                kron(0, s, half)
+            for x in range(3):
+                kron(0, x)
             spread_rows(0)
-            quant("b", 0)
-            back(0, 0)
-            back(0, 1)
-            mix(1, 0)
-            mix(1, 1)
-            product(0, 0)
+            for x in range(3, 6):
+                kron(0, x)
+            spread_rows(1)
+            interleave(0)
             turn("k", 0, 0)
             turn("k", 0, 1)
-            mix(1, 2)
-            quant("a", 0)
-            mix(1, 3)
+            quant("b", 0)
+            back(0, 0)
+            product(0, 0, 0)
+            back(0, 1)
             quant("k", 0)
-            spread_rows(1)
+            product(0, 0, 1)
+            quant("a", 0)
             for n in range(PAIRS):
                 mix(n + 2, 0)
-                back(n + 1, 0)
-                quant("b", n + 1)
                 turn("v", n + 1, 0)
-                turn("v", n + 1, 1)
+                interleave(n + 1)
+                product(n, 1, 0)
                 mix(n + 2, 1)
-                product(n, 1)
+                turn("v", n + 1, 1)
+                quant("b", n + 1)
+                product(n, 1, 1)
                 quant("v", n + 1)
+                back(n + 1, 0)
                 back(n + 1, 1)
                 mix(n + 2, 2)
                 turn("k", n + 1, 0)
-                turn("k", n + 1, 1)
-                quant("a", n + 1)
+                product(n + 1, 0, 0)
                 mix(n + 2, 3)
-                product(n + 1, 0)
+                quant("a", n + 1)
+                turn("k", n + 1, 1)
+                if n < 3:
+                    kron(1, 2 * n)
+                product(n + 1, 0, 1)
                 quant("k", n + 1)
                 if n < 3:
-                    for s, half in units[2 * n : 2 * n + 2]:
-                        kron(1, s, half)
+                    kron(1, 2 * n + 1)
                 spread_rows(n + 2)

@@ -26,9 +26,11 @@ def tile_mhla_pa_v_kernel(tc, k_feat, v, w_piece, grad_out, out_0, out_1):
         work = ctx.enter_context(tc.tile_pool(name="work", bufs=2))
         psum = ctx.enter_context(tc.psum_pool(name="psum", bufs=8))
 
-        w_all = const.tile([P, 16], BF16, name="w_all")
-        nc.scalar.dma_start(out=w_all[:], in_=w_piece.rearrange("i j -> (i j)").partition_broadcast(P))
-
+        w_rows = const.tile([P, N], BF16, name="w_rows")
+        nc.vector.memset(w_rows[:], 0.0)
+        nc.scalar.dma_start(out=w_rows[0:N, :], in_=w_piece)
+        ones = const.tile([P, P], BF16, name="ones", align_bytes=64)
+        nc.vector.memset(ones[:], 1.0)
         ident = const.tile([P, P], BF16, name="ident")
         make_identity(nc, ident[:])
         ident_f = const.tile([P, P], F32, name="ident_f")
@@ -56,8 +58,7 @@ def tile_mhla_pa_v_kernel(tc, k_feat, v, w_piece, grad_out, out_0, out_1):
             for i in range(N):
                 src = grad_out[0, h, i].rearrange("(x r) d -> r x d", r=32)
                 nc.sync.dma_start(
-                    out=g_mix[h][32 * i : 32 * i + 32, 6 * half : 6 * half + 6, :],
-                    in_=src[:, 6 * half : 6 * half + 6, :],
+                    out=g_mix[h][i:P:4, 6 * half : 6 * half + 6, :], in_=src[:, 6 * half : 6 * half + 6, :]
                 )
 
         load_kv("v", 0)
@@ -70,38 +71,51 @@ def tile_mhla_pa_v_kernel(tc, k_feat, v, w_piece, grad_out, out_0, out_1):
         load_mix(1, 0)
         load_mix(1, 1)
         load_rows(1)
-        for n in range(2, PAIRS):
+        for n in range(2, 4):
             load_kv("v", n)
             load_kv("k", n)
 
         warm = const.tile([P, 1], F32, name="warm")
         nc.vector.memset(warm[:], 0.0)
         nc.scalar.copy(out=warm[:], in_=warm[:])
-        w_f = const.tile([P, 16], F32, name="w_f")
-        nc.vector.tensor_copy(out=w_f[:], in_=w_all[:])
-        w_col = const.tile([P, N], F32, name="w_col")
-        eye = const.tile([P, 32], BF16, name="eye")
-        for i in range(4):
-            quad = slice(32 * i, 32 * i + 32)
-            nc.vector.tensor_copy(out=w_col[quad, :], in_=w_all[quad, 4 * i : 4 * i + 4])
-            nc.vector.tensor_copy(
-                out=eye[quad, :].rearrange("p (u q e) -> p q u e", u=2, e=2),
-                in_=ident[quad, quad].rearrange("p (q u e) -> p q u e", u=2, e=2),
-            )
+        eye = const.tile([P, 32], F32, name="eye")
+        nc.vector.tensor_reduce(
+            out=eye[:].rearrange("p (u q e) -> p q u e", u=2, e=2),
+            in_=ident[:].rearrange("p (q u e i) -> p q u e i", u=2, e=2, i=4),
+            axis=mybir.AxisListType.X,
+            op=ADD,
+        )
+        spread = const.tile([P, 32, N], BF16, name="spread", align_bytes=64)
+        nc.vector.tensor_copy(out=spread[:], in_=ident[:, 0:N].unsqueeze(1).to_broadcast([P, 32, N]))
         perm = const.tile([P, P], BF16, name="perm", align_bytes=64)
         nc.vector.tensor_copy(
             out=perm[:].rearrange("p (u q e) -> p q u e", u=2, e=2),
             in_=ident[:].rearrange("p (q u e) -> p q u e", u=2, e=2),
         )
+        w_diag = const.tile([P, N, N], BF16, name="w_diag")
+        for i in range(N):
+            nc.vector.tensor_scalar(
+                out=w_diag[:, i, :], in0=w_rows[:], scalar1=ident_f[:, i : i + 1], scalar2=None, op0=MULT
+            )
+        w_bank = psum.tile([P, 512], F32, name="bank")
+        nc.tensor.matmul(
+            w_bank[:, 0:16], lhsT=ones[:], rhs=w_diag[:].rearrange("p i j -> p (i j)"), start=True, stop=True
+        )
+        nc.tensor.matmul(
+            w_bank[:, 16:20], lhsT=spread[:].rearrange("p r i -> p (r i)"), rhs=w_rows[:], start=True, stop=True
+        )
+        w_f = const.tile([P, 20], F32, name="w_f")
+        nc.vector.tensor_copy(out=w_f[:], in_=w_bank[:, 0:20])
         mixer = const.tile([P, P], BF16, name="mixer", align_bytes=64)
         for j in range(N):
             nc.vector.tensor_scalar(
-                out=mixer[:, 32 * j : 32 * j + 32], in0=eye[:], scalar1=w_col[:, j : j + 1], scalar2=None, op0=MULT
+                out=mixer[:, 32 * j : 32 * j + 32], in0=eye[:], scalar1=w_f[:, 16 + j : 17 + j], scalar2=None, op0=MULT
             )
 
         mixed = [keep.tile([P, 4, N, 512], BF16, name="mixed" + str(h), align_bytes=64) for h in range(H)]
         b_in = {}
         acc = {}
+        mixed_terms = {}
         row = {}
         a_in = {}
         grouped = {}
@@ -123,23 +137,24 @@ def tile_mhla_pa_v_kernel(tc, k_feat, v, w_piece, grad_out, out_0, out_1):
         def bf16_bank():
             return psum.tile([P, 1024], BF16, name="bank")
 
-        def mix(n, i):
+        def mix(n):
             if n >= PAIRS:
                 return
+            i = mixed_terms.get(n, 0)
+            mixed_terms[n] = i + 1
             h, j = divmod(n, N)
             w_ij = w_f[:, 4 * i + j : 4 * i + j + 1]
+            src = g_row[h][:, i, :].rearrange("m (p t) -> m t p", t=4)
             if i == 0:
-                acc[n] = work.tile([P, 512], F32, name="acc", bufs=3)
+                acc[n] = work.tile([P, 4, 128], F32, name="acc", bufs=3)
                 load["v"] += 230
-                nc.vector.tensor_scalar(out=acc[n][:], in0=g_row[h][:, 0, :], scalar1=w_ij, scalar2=None, op0=MULT)
+                nc.vector.tensor_scalar(out=acc[n][:], in0=src, scalar1=w_ij, scalar2=None, op0=MULT)
                 return
             if i == 3:
-                row[n] = work.tile([P, 512], BF16, name="row", bufs=3, align_bytes=64)
+                row[n] = work.tile([P, 4, 128], BF16, name="row", bufs=3, align_bytes=64)
             dst = row[n] if i == 3 else acc[n]
             load["v"] += 480
-            nc.vector.scalar_tensor_tensor(
-                out=dst[:], in0=g_row[h][:, i, :], scalar=w_ij, in1=acc[n][:], op0=MULT, op1=ADD
-            )
+            nc.vector.scalar_tensor_tensor(out=dst[:], in0=src, scalar=w_ij, in1=acc[n][:], op0=MULT, op1=ADD)
 
         def spread_rows(n):
             if n >= PAIRS:
@@ -147,7 +162,7 @@ def tile_mhla_pa_v_kernel(tc, k_feat, v, w_piece, grad_out, out_0, out_1):
             h, j = divmod(n, N)
             bank = bf16_bank()
             for t in range(4):
-                nc.tensor.transpose(bank[:, 128 * t : 128 * t + 128], row[n][:, t:512:4], perm[:])
+                nc.tensor.transpose(bank[:, 128 * t : 128 * t + 128], row[n][:, t, :], perm[:])
             dst = mixed[h][:, :, j, :].rearrange("p t (u q) -> p t u q", u=2)
             copy_out(dst[:, :, :, 192:256], bank[:, 0:512].rearrange("p (t u q) -> p t u q", t=4, u=2), 256)
 
@@ -275,49 +290,60 @@ def tile_mhla_pa_v_kernel(tc, k_feat, v, w_piece, grad_out, out_0, out_1):
 
         with tc.manual_schedule():
             turn("v", 0, 0, "s")
+            mix(0)
+            mix(1)
+            mix(0)
+            mix(1)
+            mix(0)
             turn("v", 0, 1, "s")
-            for i in range(N):
-                mix(0, i)
-                mix(1, i)
+            mix(1)
             quant("v", 0)
-            for x in range(3):
-                kron(0, x)
+            mix(0)
+            kron(0, 0)
+            mix(1)
+            kron(0, 2)
+            kron(0, 1)
+            kron(0, 3)
             spread_rows(0)
-            for x in range(3, 6):
-                kron(0, x)
-            spread_rows(1)
+            kron(0, 4)
+            kron(0, 5)
             interleave(0)
-            turn("k", 0, 0)
-            turn("k", 0, 1)
-            quant("b", 0)
+            spread_rows(1)
             back(0, 0)
-            product(0, 0, 0)
+            turn("k", 0, 0)
+            quant("b", 0)
             back(0, 1)
+            turn("k", 0, 1)
+            quant("a", 0)
+            product(0, 0, 0)
             quant("k", 0)
             product(0, 0, 1)
-            quant("a", 0)
             for n in range(PAIRS):
-                mix(n + 2, 0)
                 turn("v", n + 1, 0)
+                mix(n + 2)
                 interleave(n + 1)
-                product(n, 1, 0)
-                mix(n + 2, 1)
+                mix(n + 2)
                 turn("v", n + 1, 1)
-                quant("b", n + 1)
-                product(n, 1, 1)
-                quant("v", n + 1)
+                if n + 4 < PAIRS:
+                    load_kv("k", n + 4)
                 back(n + 1, 0)
+                product(n, 1, 0)
+                quant("v", n + 1)
                 back(n + 1, 1)
-                mix(n + 2, 2)
+                quant("b", n + 1)
+                mix(n + 2)
+                product(n, 1, 1)
                 turn("k", n + 1, 0)
-                product(n + 1, 0, 0)
-                mix(n + 2, 3)
-                quant("a", n + 1)
-                turn("k", n + 1, 1)
                 if n < 3:
                     kron(1, 2 * n)
+                turn("k", n + 1, 1)
+                mix(n + 2)
+                product(n + 1, 0, 0)
+                quant("a", n + 1)
                 product(n + 1, 0, 1)
                 quant("k", n + 1)
                 if n < 3:
                     kron(1, 2 * n + 1)
                 spread_rows(n + 2)
+                if n + 4 < PAIRS:
+                    load_kv("v", n + 4)

@@ -40,20 +40,24 @@ def tile_mhla_pa_v_kernel(tc, k_feat, v, w_piece, grad_out, out_0, out_1):
         g_mix = {}
         g_row = {}
 
-        def load_kv(which, n):
+        def load_kv(which, n, part=None):
             h, j = divmod(n, N)
-            t = keep.tile([P, 2048], BF16, name=which + str(n), align_bytes=64)
+            if (which, n) not in raw:
+                raw[which, n] = keep.tile([P, 2048], BF16, name="raw_" + which, bufs=5, align_bytes=64)
             src = (k_feat if which == "k" else v)[0, h, j].rearrange("(m b) d -> m (b d)", b=4)
-            nc.sync.dma_start(out=t[:], in_=src)
-            raw[which, n] = t
+            cols = slice(0, 2048) if part is None else slice(1024 * part, 1024 * part + 1024)
+            nc.sync.dma_start(out=raw[which, n][:, cols], in_=src[:, cols])
 
-        def load_rows(h):
-            t = keep.tile([P, N, 512], BF16, name="g_row" + str(h), align_bytes=64)
-            nc.sync.dma_start(out=t[:], in_=grad_out[0, h].rearrange("i q d -> q i d")[384:512])
-            g_row[h] = t
+        def load_rows(h, half):
+            if h not in g_row:
+                g_row[h] = keep.tile([P, N, 512], BF16, name="g_row" + str(h), align_bytes=64)
+            i0 = 2 * half
+            nc.sync.dma_start(
+                out=g_row[h][:, i0 : i0 + 2, :], in_=grad_out[0, h].rearrange("i q d -> q i d")[384:512, i0 : i0 + 2, :]
+            )
 
         def load_mix(h, half):
-            if half == 0:
+            if h not in g_mix:
                 g_mix[h] = keep.tile([P, 12, 512], BF16, name="g_mix" + str(h), align_bytes=64)
             for i in range(N):
                 src = grad_out[0, h, i].rearrange("(x r) d -> r x d", r=32)
@@ -61,19 +65,25 @@ def tile_mhla_pa_v_kernel(tc, k_feat, v, w_piece, grad_out, out_0, out_1):
                     out=g_mix[h][i:P:4, 6 * half : 6 * half + 6, :], in_=src[:, 6 * half : 6 * half + 6, :]
                 )
 
-        load_kv("v", 0)
-        load_rows(0)
         load_mix(0, 0)
+        load_rows(0, 0)
+        load_kv("v", 0, 0)
+        load_rows(0, 1)
         load_mix(0, 1)
-        load_kv("k", 0)
+        load_kv("v", 0, 1)
         load_kv("v", 1)
+        load_kv("k", 0)
+        load_mix(1, 1)
+        load_kv("k", 2)
         load_kv("k", 1)
         load_mix(1, 0)
-        load_mix(1, 1)
-        load_rows(1)
-        for n in range(2, 4):
-            load_kv("v", n)
-            load_kv("k", n)
+        load_kv("k", 4)
+        load_kv("v", 4)
+        load_kv("v", 2)
+        load_kv("k", 3)
+        load_kv("v", 3)
+        load_rows(1, 0)
+        load_rows(1, 1)
 
         warm = const.tile([P, 1], F32, name="warm")
         nc.vector.memset(warm[:], 0.0)
@@ -93,10 +103,12 @@ def tile_mhla_pa_v_kernel(tc, k_feat, v, w_piece, grad_out, out_0, out_1):
             in_=ident[:].rearrange("p (q u e) -> p q u e", u=2, e=2),
         )
         w_diag = const.tile([P, N, N], BF16, name="w_diag")
-        for i in range(N):
-            nc.vector.tensor_scalar(
-                out=w_diag[:, i, :], in0=w_rows[:], scalar1=ident_f[:, i : i + 1], scalar2=None, op0=MULT
-            )
+        nc.vector.tensor_tensor(
+            out=w_diag[:],
+            in0=w_rows[:].unsqueeze(1).to_broadcast([P, N, N]),
+            in1=ident[:, 0:N].unsqueeze(2).to_broadcast([P, N, N]),
+            op=MULT,
+        )
         w_bank = psum.tile([P, 512], F32, name="bank")
         nc.tensor.matmul(
             w_bank[:, 0:16], lhsT=ones[:], rhs=w_diag[:].rearrange("p i j -> p (i j)"), start=True, stop=True
@@ -107,10 +119,12 @@ def tile_mhla_pa_v_kernel(tc, k_feat, v, w_piece, grad_out, out_0, out_1):
         w_f = const.tile([P, 20], F32, name="w_f")
         nc.vector.tensor_copy(out=w_f[:], in_=w_bank[:, 0:20])
         mixer = const.tile([P, P], BF16, name="mixer", align_bytes=64)
-        for j in range(N):
-            nc.vector.tensor_scalar(
-                out=mixer[:, 32 * j : 32 * j + 32], in0=eye[:], scalar1=w_f[:, 16 + j : 17 + j], scalar2=None, op0=MULT
-            )
+        nc.vector.tensor_tensor(
+            out=mixer[:].rearrange("p (j r) -> p j r", j=N),
+            in0=eye[:].unsqueeze(1).to_broadcast([P, N, 32]),
+            in1=w_f[:, 16:20].unsqueeze(2).to_broadcast([P, N, 32]),
+            op=MULT,
+        )
 
         mixed = [keep.tile([P, 4, N, 512], BF16, name="mixed" + str(h), align_bytes=64) for h in range(H)]
         b_in = {}
@@ -120,15 +134,12 @@ def tile_mhla_pa_v_kernel(tc, k_feat, v, w_piece, grad_out, out_0, out_1):
         a_in = {}
         grouped = {}
         codes = {}
-        load = {"v": 0, "s": 3000}
+        on_vector = set("mul-5 mul-6 mul-4 mul-7 rows-0 back-7-0 rows-7 k-0-0 k-7-0 out-6-0-1 out-7-0-0 v-7-0 k-3-0 out-3-1-3 k-3-1 back-5-1 out-5-1-2 v-6-1 k-1-0 rows-4 mul-0 out-1-0-0 back-2-1 out-1-0-3 out-1-1-3 out-1-1-2 out-3-1-1 out-3-0-0 mul-2 out-1-0-1 out-7-1-0".split())
 
-        def copy_out(dst, src, columns, engine=None):
-            cost = 830 * columns // 1000 + 60
-            if engine == "v" or (engine is None and load["v"] < load["s"]):
-                load["v"] += cost
+        def copy_out(dst, src, *key):
+            if "-".join(str(x) for x in key) in on_vector:
                 nc.vector.tensor_copy(out=dst, in_=src)
             else:
-                load["s"] += cost + 0
                 nc.scalar.copy(out=dst, in_=src)
 
         def f32_bank():
@@ -141,19 +152,24 @@ def tile_mhla_pa_v_kernel(tc, k_feat, v, w_piece, grad_out, out_0, out_1):
             if n >= PAIRS:
                 return
             i = mixed_terms.get(n, 0)
+            if i == N:
+                return
             mixed_terms[n] = i + 1
             h, j = divmod(n, N)
             w_ij = w_f[:, 4 * i + j : 4 * i + j + 1]
             src = g_row[h][:, i, :].rearrange("m (p t) -> m t p", t=4)
             if i == 0:
-                acc[n] = work.tile([P, 4, 128], F32, name="acc", bufs=3)
-                load["v"] += 230
-                nc.vector.tensor_scalar(out=acc[n][:], in0=src, scalar1=w_ij, scalar2=None, op0=MULT)
+                acc[n] = work.tile([P, 4, 128], F32, name="acc", bufs=4)
+                if "mul-" + str(n) in on_vector:
+                    nc.vector.tensor_scalar(out=acc[n][:], in0=src, scalar1=w_ij, scalar2=None, op0=MULT)
+                else:
+                    nc.scalar.activation(
+                        out=acc[n][:], in_=src, func=mybir.ActivationFunctionType.Copy, scale=w_ij
+                    )
                 return
             if i == 3:
-                row[n] = work.tile([P, 4, 128], BF16, name="row", bufs=3, align_bytes=64)
+                row[n] = work.tile([P, 4, 128], BF16, name="row", bufs=4, align_bytes=64)
             dst = row[n] if i == 3 else acc[n]
-            load["v"] += 480
             nc.vector.scalar_tensor_tensor(out=dst[:], in0=src, scalar=w_ij, in1=acc[n][:], op0=MULT, op1=ADD)
 
         def spread_rows(n):
@@ -164,7 +180,7 @@ def tile_mhla_pa_v_kernel(tc, k_feat, v, w_piece, grad_out, out_0, out_1):
             for t in range(4):
                 nc.tensor.transpose(bank[:, 128 * t : 128 * t + 128], row[n][:, t, :], perm[:])
             dst = mixed[h][:, :, j, :].rearrange("p t (u q) -> p t u q", u=2)
-            copy_out(dst[:, :, :, 192:256], bank[:, 0:512].rearrange("p (t u q) -> p t u q", t=4, u=2), 256)
+            copy_out(dst[:, :, :, 192:256], bank[:, 0:512].rearrange("p (t u q) -> p t u q", t=4, u=2), "rows", n)
 
         def kron(h, x):
             bank = bf16_bank()
@@ -180,7 +196,7 @@ def tile_mhla_pa_v_kernel(tc, k_feat, v, w_piece, grad_out, out_0, out_1):
                     )
             dst = mixed[h][:].rearrange("p t j (u q) -> p (t j u) q", u=2)[:, :, 32 * x : 32 * x + 32]
             copy_out(
-                dst.rearrange("p a (g y) -> p a g y", g=2), bank[:].rearrange("p (g a y) -> p a g y", g=2, y=16), 512
+                dst.rearrange("p a (g y) -> p a g y", g=2), bank[:].rearrange("p (g a y) -> p a g y", g=2, y=16), "mix", h, x
             )
 
         def interleave(n):
@@ -188,16 +204,15 @@ def tile_mhla_pa_v_kernel(tc, k_feat, v, w_piece, grad_out, out_0, out_1):
                 return
             h, j = divmod(n, N)
             b_in[n] = work.tile([P, 2048], BF16, name="b_in", align_bytes=64)
-            load["v"] += 1090
             nc.vector.tensor_copy(
                 out=b_in[n][:].rearrange("p (c i t) -> p c t i", i=4, t=4),
                 in_=mixed[h][:, :, j, :].rearrange("p t (c i) -> p c t i", i=4),
             )
 
-        def turn(which, n, half, engine=None):
+        def turn(which, n, half):
             if n >= PAIRS:
                 return
-            if half == 0:
+            if (which, n) not in grouped:
                 grouped[which, n] = work.tile([P, 2048], BF16, name="grouped_" + which, align_bytes=64)
             words = raw[which, n][:].bitcast(F32)
             bank = f32_bank()
@@ -211,8 +226,9 @@ def tile_mhla_pa_v_kernel(tc, k_feat, v, w_piece, grad_out, out_0, out_1):
             copy_out(
                 dst.rearrange("p (b m u) -> p b m u", b=2, u=2),
                 bank[:].rearrange("p (b u m) -> p b m u", b=2, u=2),
-                512,
-                engine,
+                which,
+                n,
+                half,
             )
 
         def quant(which, n):
@@ -225,9 +241,9 @@ def tile_mhla_pa_v_kernel(tc, k_feat, v, w_piece, grad_out, out_0, out_1):
                 src, fmt = a_in[n][:], E5M2
             else:
                 src, fmt = grouped[which, n][:], E4M3
-            c = work.tile([P, 512], U32, name="codes_" + which, align_bytes=64)
-            sc = work.tile([P, 512], U8, name="scales_" + which, align_bytes=64)
-            load["v"] += 480
+            depth = 2 if which in "ab" else 5
+            c = work.tile([P, 512], U32, name="codes_" + which, bufs=depth, align_bytes=64)
+            sc = work.tile([P, 512], U8, name="scales_" + which, bufs=depth, align_bytes=64)
             nc.vector.quantize_mx(out=c[:].bitcast(fmt), scales=sc[:], in_=src)
             codes[which, n] = (c, sc)
 
@@ -235,7 +251,7 @@ def tile_mhla_pa_v_kernel(tc, k_feat, v, w_piece, grad_out, out_0, out_1):
             if n >= PAIRS:
                 return
             h, j = divmod(n, N)
-            if half == 0:
+            if n not in a_in:
                 a_in[n] = work.tile([P, 2048], BF16, name="a_in", align_bytes=64)
             words = mixed[h][:].rearrange("p t j c -> p (t j c)").bitcast(F32)
             bank = f32_bank()
@@ -248,7 +264,9 @@ def tile_mhla_pa_v_kernel(tc, k_feat, v, w_piece, grad_out, out_0, out_1):
             copy_out(
                 dst.rearrange("q (t p u) -> q t p u", t=2, u=2),
                 bank[:].rearrange("q (t u p) -> q t p u", t=2, u=2),
-                512,
+                "back",
+                n,
+                half,
             )
 
         results = {}
@@ -282,68 +300,98 @@ def tile_mhla_pa_v_kernel(tc, k_feat, v, w_piece, grad_out, out_0, out_1):
                 else:
                     dst = res[:, b, :].rearrange("m (p t) -> m p t", t=4)
                     src = bank[:].rearrange("m (t p) -> m p t", t=4)
-                copy_out(dst, src, 512)
+                copy_out(dst, src, "out", n, which, b)
                 if n == PAIRS - 1 and which == 1:
                     nc.sync.dma_start(out=view[:, b, :], in_=res[:, b, :])
             if not (n == PAIRS - 1 and which == 1):
                 nc.sync.dma_start(out=view[:, 2 * pair : 2 * pair + 2, :], in_=res[:, 2 * pair : 2 * pair + 2, :])
 
         with tc.manual_schedule():
-            turn("v", 0, 0, "s")
-            mix(0)
+            mix(2)
+            mix(3)
+            mix(2)
             mix(1)
-            mix(0)
-            mix(1)
-            mix(0)
-            turn("v", 0, 1, "s")
-            mix(1)
-            quant("v", 0)
-            mix(0)
+            kron(0, 1)
+            kron(0, 2)
+            turn("v", 0, 0)
+            kron(0, 3)
             kron(0, 0)
             mix(1)
-            kron(0, 2)
-            kron(0, 1)
-            kron(0, 3)
-            spread_rows(0)
-            kron(0, 4)
+            mix(0)
+            mix(0)
+            turn("v", 0, 1)
+            mix(2)
+            mix(3)
+            mix(3)
+            mix(1)
+            mix(1)
+            mix(0)
             kron(0, 5)
-            interleave(0)
-            spread_rows(1)
+            kron(0, 4)
+            mix(0)
+            quant("v", 0)
+            spread_rows(0)
             back(0, 0)
-            turn("k", 0, 0)
-            quant("b", 0)
+            interleave(0)
             back(0, 1)
-            turn("k", 0, 1)
+            spread_rows(1)
+            quant("b", 0)
+            turn("k", 0, 0)
             quant("a", 0)
+            turn("k", 0, 1)
             product(0, 0, 0)
             quant("k", 0)
             product(0, 0, 1)
-            for n in range(PAIRS):
+            mix(3)
+            for n in range(3):
+                mix(n + 2)
+                mix(n + 2)
+                turn("v", n + 1, 1)
+                turn("v", n + 1, 0)
+                back(n + 1, 0)
+                interleave(n + 1)
+                product(n, 1, 0)
+                mix(n + 2)
+                quant("b", n + 1)
+                quant("v", n + 1)
+                back(n + 1, 1)
+                turn("k", n + 1, 0)
+                turn("k", n + 1, 1)
+                product(n, 1, 1)
+                mix(n + 2)
+                if n + 5 < PAIRS:
+                    load_kv("v", n + 5)
+                product(n + 1, 0, 0)
+                quant("k", n + 1)
+                quant("a", n + 1)
+                product(n + 1, 0, 1)
+                spread_rows(n + 2)
+                kron(1, 2 * n)
+                if n + 5 < PAIRS:
+                    load_kv("k", n + 5)
+                kron(1, 2 * n + 1)
+            for n in range(3, PAIRS):
+                mix(n + 2)
+                mix(n + 2)
+                turn("v", n + 1, 1)
                 turn("v", n + 1, 0)
                 mix(n + 2)
                 interleave(n + 1)
-                mix(n + 2)
-                turn("v", n + 1, 1)
-                if n + 4 < PAIRS:
-                    load_kv("k", n + 4)
-                back(n + 1, 0)
                 product(n, 1, 0)
+                if n + 5 < PAIRS:
+                    load_kv("k", n + 5)
                 quant("v", n + 1)
-                back(n + 1, 1)
                 quant("b", n + 1)
+                turn("k", n + 1, 1)
+                back(n + 1, 0)
+                turn("k", n + 1, 0)
                 mix(n + 2)
                 product(n, 1, 1)
-                turn("k", n + 1, 0)
-                if n < 3:
-                    kron(1, 2 * n)
-                turn("k", n + 1, 1)
-                mix(n + 2)
+                back(n + 1, 1)
                 product(n + 1, 0, 0)
-                quant("a", n + 1)
-                product(n + 1, 0, 1)
                 quant("k", n + 1)
-                if n < 3:
-                    kron(1, 2 * n + 1)
+                quant("a", n + 1)
+                if n + 5 < PAIRS:
+                    load_kv("v", n + 5)
                 spread_rows(n + 2)
-                if n + 4 < PAIRS:
-                    load_kv("v", n + 4)
+                product(n + 1, 0, 1)

from contextlib import ExitStack

import concourse.mybir as mybir
from concourse.masks import make_identity

F32 = mybir.dt.float32
BF16 = mybir.dt.bfloat16
U32 = mybir.dt.uint32
U8 = mybir.dt.uint8
E4M3 = mybir.dt.float8_e4m3fn_x4
E5M2 = mybir.dt.float8_e5m2_x4
MULT = mybir.AluOpType.mult
ADD = mybir.AluOpType.add

H, N, W, D = 2, 4, 512, 512
P = 128
PAIRS = H * N
FLOPS = 2 * 2 * PAIRS * W * D * D


def tile_mhla_pa_v_kernel(tc, k_feat, v, w_piece, grad_out, out_0, out_1):
    nc = tc.nc
    with ExitStack() as ctx:
        const = ctx.enter_context(tc.tile_pool(name="const", bufs=1))
        keep = ctx.enter_context(tc.tile_pool(name="keep", bufs=1))
        work = ctx.enter_context(tc.tile_pool(name="work", bufs=2))
        psum = ctx.enter_context(tc.psum_pool(name="psum", bufs=8))

        w_rows = const.tile([P, N], BF16, name="w_rows")
        nc.vector.memset(w_rows[:], 0.0)
        nc.scalar.dma_start(out=w_rows[0:N, :], in_=w_piece)
        ones = const.tile([P, P], BF16, name="ones", align_bytes=64)
        nc.vector.memset(ones[:], 1.0)
        ident = const.tile([P, P], BF16, name="ident")
        make_identity(nc, ident[:])
        ident_f = const.tile([P, P], F32, name="ident_f")
        make_identity(nc, ident_f[:])

        raw = {}
        g_mix = {}
        g_row = {}

        def load_kv(which, n, part=None):
            h, j = divmod(n, N)
            if (which, n) not in raw:
                raw[which, n] = keep.tile([P, 2048], BF16, name="raw_" + which, bufs=5, align_bytes=64)
            src = (k_feat if which == "k" else v)[0, h, j].rearrange("(m b) d -> m (b d)", b=4)
            cols = slice(0, 2048) if part is None else slice(1024 * part, 1024 * part + 1024)
            nc.sync.dma_start(out=raw[which, n][:, cols], in_=src[:, cols])

        def load_rows(h, half):
            if h not in g_row:
                g_row[h] = keep.tile([P, N, 512], BF16, name="g_row" + str(h), align_bytes=64)
            i0 = 2 * half
            nc.sync.dma_start(
                out=g_row[h][:, i0 : i0 + 2, :], in_=grad_out[0, h].rearrange("i q d -> q i d")[384:512, i0 : i0 + 2, :]
            )

        def load_mix(h, half):
            if h not in g_mix:
                g_mix[h] = keep.tile([P, 12, 512], BF16, name="g_mix" + str(h), align_bytes=64)
            for i in range(N):
                src = grad_out[0, h, i].rearrange("(x r) d -> r x d", r=32)
                nc.sync.dma_start(
                    out=g_mix[h][i:P:4, 6 * half : 6 * half + 6, :], in_=src[:, 6 * half : 6 * half + 6, :]
                )

        load_mix(0, 0)
        load_rows(0, 0)
        load_kv("v", 0, 0)
        load_rows(0, 1)
        load_mix(0, 1)
        load_kv("v", 0, 1)
        load_kv("v", 1)
        load_kv("k", 0)
        load_mix(1, 1)
        load_kv("k", 2)
        load_kv("k", 1)
        load_mix(1, 0)
        load_kv("k", 4)
        load_kv("v", 4)
        load_kv("v", 2)
        load_kv("k", 3)
        load_kv("v", 3)
        load_rows(1, 0)
        load_rows(1, 1)

        warm = const.tile([P, 1], F32, name="warm")
        nc.vector.memset(warm[:], 0.0)
        nc.scalar.copy(out=warm[:], in_=warm[:])
        eye = const.tile([P, 32], F32, name="eye")
        nc.vector.tensor_reduce(
            out=eye[:].rearrange("p (u q e) -> p q u e", u=2, e=2),
            in_=ident[:].rearrange("p (q u e i) -> p q u e i", u=2, e=2, i=4),
            axis=mybir.AxisListType.X,
            op=ADD,
        )
        spread = const.tile([P, 32, N], BF16, name="spread", align_bytes=64)
        nc.vector.tensor_copy(out=spread[:], in_=ident[:, 0:N].unsqueeze(1).to_broadcast([P, 32, N]))
        perm = const.tile([P, P], BF16, name="perm", align_bytes=64)
        nc.vector.tensor_copy(
            out=perm[:].rearrange("p (u q e) -> p q u e", u=2, e=2),
            in_=ident[:].rearrange("p (q u e) -> p q u e", u=2, e=2),
        )
        w_diag = const.tile([P, N, N], BF16, name="w_diag")
        nc.vector.tensor_tensor(
            out=w_diag[:],
            in0=w_rows[:].unsqueeze(1).to_broadcast([P, N, N]),
            in1=ident[:, 0:N].unsqueeze(2).to_broadcast([P, N, N]),
            op=MULT,
        )
        w_bank = psum.tile([P, 512], F32, name="bank")
        nc.tensor.matmul(
            w_bank[:, 0:16], lhsT=ones[:], rhs=w_diag[:].rearrange("p i j -> p (i j)"), start=True, stop=True
        )
        nc.tensor.matmul(
            w_bank[:, 16:20], lhsT=spread[:].rearrange("p r i -> p (r i)"), rhs=w_rows[:], start=True, stop=True
        )
        w_f = const.tile([P, 20], F32, name="w_f")
        nc.vector.tensor_copy(out=w_f[:], in_=w_bank[:, 0:20])
        mixer = const.tile([P, P], BF16, name="mixer", align_bytes=64)
        nc.vector.tensor_tensor(
            out=mixer[:].rearrange("p (j r) -> p j r", j=N),
            in0=eye[:].unsqueeze(1).to_broadcast([P, N, 32]),
            in1=w_f[:, 16:20].unsqueeze(2).to_broadcast([P, N, 32]),
            op=MULT,
        )

        mixed = [keep.tile([P, 4, N, 512], BF16, name="mixed" + str(h), align_bytes=64) for h in range(H)]
        b_in = {}
        acc = {}
        mixed_terms = {}
        row = {}
        a_in = {}
        grouped = {}
        codes = {}
        on_vector = set("mul-5 mul-6 mul-4 mul-7 rows-0 back-7-0 rows-7 k-0-0 k-7-0 out-6-0-1 out-7-0-0 v-7-0 k-3-0 out-3-1-3 k-3-1 back-5-1 out-5-1-2 v-6-1 k-1-0 rows-4 mul-0 out-1-0-0 back-2-1 out-1-0-3 out-1-1-3 out-1-1-2 out-3-1-1 out-3-0-0 mul-2 out-1-0-1 out-7-1-0".split())

        def copy_out(dst, src, *key):
            if "-".join(str(x) for x in key) in on_vector:
                nc.vector.tensor_copy(out=dst, in_=src)
            else:
                nc.scalar.copy(out=dst, in_=src)

        def f32_bank():
            return psum.tile([P, 512], F32, name="bank")

        def bf16_bank():
            return psum.tile([P, 1024], BF16, name="bank")

        def mix(n):
            if n >= PAIRS:
                return
            i = mixed_terms.get(n, 0)
            if i == N:
                return
            mixed_terms[n] = i + 1
            h, j = divmod(n, N)
            w_ij = w_f[:, 4 * i + j : 4 * i + j + 1]
            src = g_row[h][:, i, :].rearrange("m (p t) -> m t p", t=4)
            if i == 0:
                acc[n] = work.tile([P, 4, 128], F32, name="acc", bufs=4)
                if "mul-" + str(n) in on_vector:
                    nc.vector.tensor_scalar(out=acc[n][:], in0=src, scalar1=w_ij, scalar2=None, op0=MULT)
                else:
                    nc.scalar.activation(
                        out=acc[n][:], in_=src, func=mybir.ActivationFunctionType.Copy, scale=w_ij
                    )
                return
            if i == 3:
                row[n] = work.tile([P, 4, 128], BF16, name="row", bufs=4, align_bytes=64)
            dst = row[n] if i == 3 else acc[n]
            nc.vector.scalar_tensor_tensor(out=dst[:], in0=src, scalar=w_ij, in1=acc[n][:], op0=MULT, op1=ADD)

        def spread_rows(n):
            if n >= PAIRS:
                return
            h, j = divmod(n, N)
            bank = bf16_bank()
            for t in range(4):
                nc.tensor.transpose(bank[:, 128 * t : 128 * t + 128], row[n][:, t, :], perm[:])
            dst = mixed[h][:, :, j, :].rearrange("p t (u q) -> p t u q", u=2)
            copy_out(dst[:, :, :, 192:256], bank[:, 0:512].rearrange("p (t u q) -> p t u q", t=4, u=2), "rows", n)

        def kron(h, x):
            bank = bf16_bank()
            for g in range(2):
                for t in range(4):
                    c0 = 512 * g + 128 * t
                    nc.tensor.matmul(
                        bank[:, c0 : c0 + 128],
                        lhsT=g_mix[h][:, 2 * x + g, t:512:4],
                        rhs=mixer[:],
                        start=True,
                        stop=True,
                    )
            dst = mixed[h][:].rearrange("p t j (u q) -> p (t j u) q", u=2)[:, :, 32 * x : 32 * x + 32]
            copy_out(
                dst.rearrange("p a (g y) -> p a g y", g=2), bank[:].rearrange("p (g a y) -> p a g y", g=2, y=16), "mix", h, x
            )

        def interleave(n):
            if n >= PAIRS:
                return
            h, j = divmod(n, N)
            b_in[n] = work.tile([P, 2048], BF16, name="b_in", align_bytes=64)
            nc.vector.tensor_copy(
                out=b_in[n][:].rearrange("p (c i t) -> p c t i", i=4, t=4),
                in_=mixed[h][:, :, j, :].rearrange("p t (c i) -> p c t i", i=4),
            )

        def turn(which, n, half):
            if n >= PAIRS:
                return
            if (which, n) not in grouped:
                grouped[which, n] = work.tile([P, 2048], BF16, name="grouped_" + which, align_bytes=64)
            words = raw[which, n][:].bitcast(F32)
            bank = f32_bank()
            for b in range(2):
                for u in range(2):
                    w0 = 256 * (2 * half + b)
                    nc.tensor.transpose(
                        bank[:, 256 * b + 128 * u : 256 * b + 128 * u + 128], words[:, w0 + u : w0 + 256 : 2], ident_f[:]
                    )
            dst = grouped[which, n][:].bitcast(F32)[:, 512 * half : 512 * half + 512]
            copy_out(
                dst.rearrange("p (b m u) -> p b m u", b=2, u=2),
                bank[:].rearrange("p (b u m) -> p b m u", b=2, u=2),
                which,
                n,
                half,
            )

        def quant(which, n):
            if n >= PAIRS:
                return
            h, j = divmod(n, N)
            if which == "b":
                src, fmt = b_in[n][:], E5M2
            elif which == "a":
                src, fmt = a_in[n][:], E5M2
            else:
                src, fmt = grouped[which, n][:], E4M3
            depth = 2 if which in "ab" else 5
            c = work.tile([P, 512], U32, name="codes_" + which, bufs=depth, align_bytes=64)
            sc = work.tile([P, 512], U8, name="scales_" + which, bufs=depth, align_bytes=64)
            nc.vector.quantize_mx(out=c[:].bitcast(fmt), scales=sc[:], in_=src)
            codes[which, n] = (c, sc)

        def back(n, half):
            if n >= PAIRS:
                return
            h, j = divmod(n, N)
            if n not in a_in:
                a_in[n] = work.tile([P, 2048], BF16, name="a_in", align_bytes=64)
            words = mixed[h][:].rearrange("p t j c -> p (t j c)").bitcast(F32)
            bank = f32_bank()
            for tt in range(2):
                for u in range(2):
                    c0 = 256 * tt + 128 * u
                    w0 = 256 * (N * (2 * half + tt) + j) + 128 * u
                    nc.tensor.transpose(bank[:, c0 : c0 + 128], words[:, w0 : w0 + 128], ident_f[:])
            dst = a_in[n][:].bitcast(F32)[:, 512 * half : 512 * half + 512]
            copy_out(
                dst.rearrange("q (t p u) -> q t p u", t=2, u=2),
                bank[:].rearrange("q (t u p) -> q t p u", t=2, u=2),
                "back",
                n,
                half,
            )

        results = {}

        def product(n, which, pair):
            if n >= PAIRS:
                return
            h, j = divmod(n, N)
            left, right, dram = ("v", "b", out_0) if which == 0 else ("k", "a", out_1)
            lc, ls = codes[left, n]
            rc, rs = codes[right, n]
            if pair == 0:
                results[which] = work.tile([P, 4, 512], F32, name="res" + str(which))
            res = results[which]
            view = dram[0, h, j].rearrange("(m b) d -> m b d", b=4)
            for b in range(2 * pair, 2 * pair + 2):
                bank = f32_bank()
                cols = slice(128 * b, 128 * b + 128)
                nc.tensor.matmul_mx(
                    out=bank[:],
                    lhsT=lc[:, cols].bitcast(E4M3),
                    lhsT_scale=ls[:, cols],
                    rhs=rc[:].bitcast(E5M2),
                    rhs_scale=rs[:],
                    start=True,
                    stop=True,
                )
                if which == 0:
                    dst = res[:, b, :].rearrange("m (q u e) -> m q u e", u=2, e=2)
                    src = bank[:].rearrange("m (u q e) -> m q u e", u=2, e=2)
                else:
                    dst = res[:, b, :].rearrange("m (p t) -> m p t", t=4)
                    src = bank[:].rearrange("m (t p) -> m p t", t=4)
                copy_out(dst, src, "out", n, which, b)
                if n == PAIRS - 1 and which == 1:
                    nc.sync.dma_start(out=view[:, b, :], in_=res[:, b, :])
            if not (n == PAIRS - 1 and which == 1):
                nc.sync.dma_start(out=view[:, 2 * pair : 2 * pair + 2, :], in_=res[:, 2 * pair : 2 * pair + 2, :])

        with tc.manual_schedule():
            mix(2)
            mix(3)
            mix(2)
            mix(1)
            kron(0, 1)
            kron(0, 2)
            turn("v", 0, 0)
            kron(0, 3)
            kron(0, 0)
            mix(1)
            mix(0)
            mix(0)
            turn("v", 0, 1)
            mix(2)
            mix(3)
            mix(3)
            mix(1)
            mix(1)
            mix(0)
            kron(0, 5)
            kron(0, 4)
            mix(0)
            quant("v", 0)
            spread_rows(0)
            back(0, 0)
            interleave(0)
            back(0, 1)
            spread_rows(1)
            quant("b", 0)
            turn("k", 0, 0)
            quant("a", 0)
            turn("k", 0, 1)
            product(0, 0, 0)
            quant("k", 0)
            product(0, 0, 1)
            mix(3)
            for n in range(3):
                mix(n + 2)
                mix(n + 2)
                turn("v", n + 1, 1)
                turn("v", n + 1, 0)
                back(n + 1, 0)
                interleave(n + 1)
                product(n, 1, 0)
                mix(n + 2)
                quant("b", n + 1)
                quant("v", n + 1)
                back(n + 1, 1)
                turn("k", n + 1, 0)
                turn("k", n + 1, 1)
                product(n, 1, 1)
                mix(n + 2)
                if n + 5 < PAIRS:
                    load_kv("v", n + 5)
                product(n + 1, 0, 0)
                quant("k", n + 1)
                quant("a", n + 1)
                product(n + 1, 0, 1)
                spread_rows(n + 2)
                kron(1, 2 * n)
                if n + 5 < PAIRS:
                    load_kv("k", n + 5)
                kron(1, 2 * n + 1)
            for n in range(3, PAIRS):
                mix(n + 2)
                mix(n + 2)
                turn("v", n + 1, 1)
                turn("v", n + 1, 0)
                mix(n + 2)
                interleave(n + 1)
                product(n, 1, 0)
                if n + 5 < PAIRS:
                    load_kv("k", n + 5)
                quant("v", n + 1)
                quant("b", n + 1)
                turn("k", n + 1, 1)
                back(n + 1, 0)
                turn("k", n + 1, 0)
                mix(n + 2)
                product(n, 1, 1)
                back(n + 1, 1)
                product(n + 1, 0, 0)
                quant("k", n + 1)
                quant("a", n + 1)
                if n + 5 < PAIRS:
                    load_kv("v", n + 5)
                spread_rows(n + 2)
                product(n + 1, 0, 1)
